import numpy as np
import ml_dtypes


def mxq(x, axis, fmt="e4m3"):
    dtype, down = {"e4m3": (ml_dtypes.float8_e4m3fn, 7), "e5m2": (ml_dtypes.float8_e5m2, 14)}[fmt]
    v = np.moveaxis(np.asarray(x, np.float32).astype(ml_dtypes.bfloat16).astype(np.float64), axis, -1)
    blocks = v.reshape(v.shape[:-1] + (-1, 32))
    amax = np.abs(blocks).max(-1, keepdims=True)
    byte = np.maximum(np.where(amax > 0, np.frexp(amax)[1] - 1 + 127, 0) - down, 1)
    scale = np.exp2(byte - 127.0)
    codes = (blocks / scale).astype(np.float32).astype(dtype).astype(np.float64)
    return np.moveaxis((codes * scale).reshape(v.shape), -1, axis)


WIDE = False


def mx_kscale(k):
    if not WIDE:
        return np.ones(k)
    levels = np.array([10, -10, 5, -5, 0])
    a = np.random.permutation(np.resize(levels, k // 512 * 4)).reshape(k // 512, 4)
    idx = np.arange(k)
    return np.exp2(a[idx // 512, idx % 128 // 32])


BF16 = ml_dtypes.bfloat16


def bf(x):
    return np.asarray(x, np.float32).astype(BF16)


def f64(x):
    return np.asarray(x).astype(np.float64)


B, N, HH, WW, TC, IC, DQK = 3, 256, 32, 32, 1024, 1024, 512
M = HH * WW
BSIG = 2.0


def setup_inputs():
    s = mx_kscale(IC)
    z = np.random.standard_normal((B, N, M)) * BSIG
    e = np.exp(z - z.max(-1, keepdims=True))
    keep = np.random.uniform(size=(B, N, M)) > 0.2
    return {"beta": bf(e / e.sum(-1, keepdims=True) * keep),
            "x2": bf(np.random.standard_normal((B, HH, WW, IC)) * s),
            "Wv": bf(np.random.standard_normal((IC, TC)) * 2.0 / np.sqrt(IC) / s[:, None]),
            "bv": bf(np.random.standard_normal(TC) * 0.25)}


def reference(beta, x2, Wv, bv):
    v = (mxq(f64(x2).reshape(B, M, IC), 2, "e4m3") @ mxq(f64(Wv), 0, "e4m3")) + f64(bv)
    return mxq(f64(beta), 2, "e4m3") @ mxq(v, 1, "e4m3")

@@ -1,0 +1,254 @@
+from contextlib import ExitStack
+
+import concourse.mybir as mybir
+from concourse.masks import make_identity
+
+FLOPS = 2 * 3 * 1024 * 1024 * 1024 + 2 * 3 * 256 * 1024 * 1024
+
+BF16 = mybir.dt.bfloat16
+F32 = mybir.dt.float32
+U32 = mybir.dt.uint32
+U8 = mybir.dt.uint8
+FP8X4 = mybir.dt.float8_e4m3fn_x4
+ADD = mybir.AluOpType.add
+
+P = 128
+BATCH = 3
+IC = 1024
+TC = 1024
+W_SPLIT = 640
+
+
+def tile_text2imgca_pb_kernel(tc, beta, x2, Wv, bv, out):
+    nc = tc.nc
+    x2p = x2.rearrange("b h w c -> b (h w) c")
+    with ExitStack() as ctx:
+        keep = ctx.enter_context(tc.tile_pool(name="keep", bufs=1))
+        xgp = ctx.enter_context(tc.tile_pool(name="xgp", bufs=2))
+        xcp = ctx.enter_context(tc.tile_pool(name="xcp", bufs=2))
+        vgp = ctx.enter_context(tc.tile_pool(name="vgp", bufs=4))
+        otp = ctx.enter_context(tc.tile_pool(name="otp", bufs=4))
+        psum = ctx.enter_context(tc.psum_pool(name="psum", bufs=8))
+        ctx.enter_context(tc.manual_schedule())
+
+        def new_bank(name):
+            return psum.tile([P, 512], F32, name=name, tag="bank")
+
+        brow = keep.tile([P, TC], BF16, name="brow")
+        nc.vector.memset(brow[:], 0.0)
+        nc.sync.dma_start(out=brow[0:1, :], in_=bv.rearrange("(o c) -> o c", o=1))
+        ones = keep.tile([P, P], BF16, name="ones")
+        nc.vector.memset(ones[:], 1.0)
+        ident = keep.tile([P, P], F32, name="ident")
+        make_identity(nc, ident[:])
+
+        wr = []
+        for kg in range(2):
+            t = keep.tile([P, 4, TC], BF16, name="wr%d" % kg)
+            nc.sync.dma_start(
+                out=t[:].rearrange("p (ku ke) c -> p ku (ke c)", ku=2),
+                in_=Wv[512 * kg : 512 * (kg + 1), :].rearrange("(ku q ke) c -> q ku (ke c)", ku=2, ke=2),
+            )
+            wr.append(t)
+
+        xr = [keep.tile([P, 4, IC], BF16, name="xr%d" % hh) for hh in range(6)]
+        br = [keep.tile([P, 2, 1024], BF16, name="br%d" % b) for b in range(BATCH)]
+
+        def load_x(hh, pieces):
+            b, g = divmod(hh, 2)
+            rows = x2p[b, 512 * g : 512 * (g + 1), :]
+            if pieces == 2:
+                for u in range(2):
+                    nc.sync.dma_start(
+                        out=xr[hh][:, 2 * u : 2 * u + 2, :].rearrange("p e c -> p (e c)"),
+                        in_=rows[256 * u : 256 * (u + 1), :].rearrange("(p e) c -> p (e c)", e=2),
+                    )
+            else:
+                nc.sync.dma_start(
+                    out=xr[hh][:].rearrange("p (u e) c -> p u (e c)", u=2),
+                    in_=rows.rearrange("(u p e) c -> p u (e c)", u=2, e=2),
+                )
+
+        def load_beta(b):
+            nc.sync.dma_start(out=br[b][:], in_=beta[b].rearrange("(nt n) k -> n nt k", nt=2))
+
+        load_x(0, 2)
+        load_x(1, 1)
+        load_beta(0)
+        load_x(2, 1)
+        load_x(3, 1)
+        load_beta(1)
+        load_x(4, 1)
+        load_x(5, 1)
+        load_beta(2)
+
+        bias = keep.tile([P, TC], F32, name="bias")
+        for h in range(2):
+            pb = new_bank("pb%d" % h)
+            nc.tensor.matmul(out=pb[:], lhsT=ones[:], rhs=brow[:, 512 * h : 512 * (h + 1)], start=True, stop=True)
+            nc.scalar.copy(out=bias[:, 512 * h : 512 * (h + 1)], in_=pb[:])
+
+        wg = [keep.tile([P, TC, 4], BF16, name="wg%d" % kg, align_bytes=64) for kg in range(2)]
+        wc = [keep.tile([P, TC], U32, name="wc%d" % kg, align_bytes=64) for kg in range(2)]
+        ws = [keep.tile([P, TC], U8, name="ws%d" % kg, align_bytes=64) for kg in range(2)]
+
+        def regroup_w(kg, c0, c1, copy):
+            copy(
+                out=wg[kg][:, c0:c1, :].rearrange("p (c i) t -> p c t i", i=4),
+                in_=wr[kg][:, :, c0:c1].rearrange("p t (c i) -> p c t i", i=4),
+            )
+
+        def quant_w(kg, h):
+            cols = slice(512 * h, 512 * (h + 1))
+            nc.vector.quantize_mx(
+                out=wc[kg][:, cols].bitcast(FP8X4),
+                scales=ws[kg][:, cols],
+                in_=wg[kg][:, cols, :].rearrange("p c t -> p (c t)"),
+            )
+
+        for kg in range(2):
+            regroup_w(kg, 0, W_SPLIT, nc.vector.tensor_copy)
+            regroup_w(kg, W_SPLIT, TC, nc.scalar.copy)
+            quant_w(kg, 0)
+            quant_w(kg, 1)
+
+        xg = {}
+        xc = {}
+        xs = {}
+
+        def transpose_x(hh):
+            xg[hh] = xgp.tile([P, 4096], BF16, name="xg%d" % hh, tag="xg", align_bytes=64)
+            xc[hh] = xcp.tile([P, 1024], U32, name="xc%d" % hh, tag="xc", align_bytes=64)
+            xs[hh] = xcp.tile([P, 1024], U8, name="xs%d" % hh, tag="xs", align_bytes=64)
+            src = xr[hh][:].bitcast(F32)
+            dst = xg[hh][:].bitcast(F32)
+            for j in range(4):
+                bank = new_bank("xt%d_%d" % (hh, j))
+                for s in range(4):
+                    nc.tensor.transpose(
+                        out=bank[:, 128 * s : 128 * (s + 1)],
+                        in_=src[:, j, 128 * s : 128 * (s + 1)],
+                        identity=ident[:],
+                    )
+                nc.scalar.copy(
+                    out=dst[:, 512 * j : 512 * (j + 1)].rearrange("p (kg r ku) -> p kg r ku", kg=2, ku=2),
+                    in_=bank[:].rearrange("p (kg ku r) -> p kg r ku", kg=2, ku=2),
+                )
+
+        def quant_x(hh, part):
+            nc.vector.quantize_mx(
+                out=xc[hh][:, 512 * part : 512 * (part + 1)].bitcast(FP8X4),
+                scales=xs[hh][:, 512 * part : 512 * (part + 1)],
+                in_=xg[hh][:, 2048 * part : 2048 * (part + 1)],
+            )
+
+        bg = [keep.tile([P, 2048], BF16, name="bg%d" % b, align_bytes=64) for b in range(BATCH)]
+        bc = [keep.tile([P, 512], U32, name="bc%d" % b, align_bytes=64) for b in range(BATCH)]
+        bs = [keep.tile([P, 512], U8, name="bs%d" % b, align_bytes=64) for b in range(BATCH)]
+
+        def transpose_beta(b):
+            src = br[b][:].bitcast(F32)
+            dst = bg[b][:].bitcast(F32).rearrange("p (g nt n u) -> p g nt n u", g=2, nt=2, u=2)
+            for nt in range(2):
+                bank = new_bank("bt%d_%d" % (b, nt))
+                for s in range(4):
+                    nc.tensor.transpose(
+                        out=bank[:, 128 * s : 128 * (s + 1)],
+                        in_=src[:, nt, 128 * s : 128 * (s + 1)],
+                        identity=ident[:],
+                    )
+                nc.scalar.copy(
+                    out=dst[:, :, nt, :, :],
+                    in_=bank[:].rearrange("p (g u n) -> p g n u", g=2, u=2),
+                )
+
+        def quant_beta(b):
+            nc.vector.quantize_mx(out=bc[b][:].bitcast(FP8X4), scales=bs[b][:], in_=bg[b][:])
+
+        vg = {}
+        vc = {}
+        vs = {}
+        for hh in range(6):
+            for h in range(2):
+                vc[(hh, h)] = keep.tile([P, 512], U32, name="vc%d_%d" % (hh, h), align_bytes=64)
+                vs[(hh, h)] = keep.tile([P, 512], U8, name="vs%d_%d" % (hh, h), align_bytes=64)
+
+        def stage1(hh, c):
+            bank = new_bank("s1_%d_%d" % (hh, c))
+            cols = slice(128 * c, 128 * (c + 1))
+            for j in range(4):
+                for kg in range(2):
+                    sl = slice(128 * (2 * j + kg), 128 * (2 * j + kg + 1))
+                    nc.tensor.matmul_mx(
+                        out=bank[:, 128 * j : 128 * (j + 1)],
+                        lhsT=xc[hh][:, sl].bitcast(FP8X4),
+                        lhsT_scale=xs[hh][:, sl],
+                        rhs=wc[kg][:, cols].bitcast(FP8X4),
+                        rhs_scale=ws[kg][:, cols],
+                        start=(kg == 0),
+                        stop=(kg == 1),
+                    )
+            vg[(hh, c)] = vgp.tile([P, 512], BF16, name="vg%d_%d" % (hh, c), tag="vg", align_bytes=64)
+            nc.vector.tensor_tensor(
+                out=vg[(hh, c)][:].rearrange("p (w j) -> p w j", j=4),
+                in0=bank[:].rearrange("p (j w) -> p w j", j=4),
+                in1=bias[:, cols].unsqueeze(2).to_broadcast([P, 128, 4]),
+                op=ADD,
+            )
+
+        def quant_v(hh, c):
+            h, q = divmod(c, 4)
+            nc.vector.quantize_mx(
+                out=vc[(hh, h)][:, 128 * q : 128 * (q + 1)].bitcast(FP8X4),
+                scales=vs[(hh, h)][:, 128 * q : 128 * (q + 1)],
+                in_=vg[(hh, c)][:],
+            )
+
+        def stage2(b, nt, h, copy):
+            bank = new_bank("s2_%d_%d_%d" % (b, nt, h))
+            for g in range(2):
+                sl = slice(128 * (2 * g + nt), 128 * (2 * g + nt + 1))
+                nc.tensor.matmul_mx(
+                    out=bank[:],
+                    lhsT=bc[b][:, sl].bitcast(FP8X4),
+                    lhsT_scale=bs[b][:, sl],
+                    rhs=vc[(2 * b + g, h)][:].bitcast(FP8X4),
+                    rhs_scale=vs[(2 * b + g, h)][:],
+                    start=(g == 0),
+                    stop=(g == 1),
+                )
+            ot = otp.tile([P, 512], F32, name="ot%d_%d_%d" % (b, nt, h), tag="ot")
+            copy(out=ot[:], in_=bank[:])
+            nc.sync.dma_start(out=out[b, 128 * nt : 128 * (nt + 1), 512 * h : 512 * (h + 1)], in_=ot[:])
+
+        transpose_x(0)
+        quant_x(0, 0)
+        quant_x(0, 1)
+        waiting = []
+        for hh in range(6):
+            b, g = divmod(hh, 2)
+            for c in range(8):
+                stage1(hh, c)
+                if waiting:
+                    quant_v(waiting[0][0], waiting[0][1])
+                waiting = [(hh, c)]
+                if g == 0 and b > 0:
+                    if c == 0 or c == 1:
+                        stage2(b - 1, c, 0, nc.scalar.copy)
+                    if c == 3 or c == 4:
+                        stage2(b - 1, c - 3, 1, nc.scalar.copy)
+                if c == 1 and hh < 5:
+                    transpose_x(hh + 1)
+                    if g == 0:
+                        transpose_beta(b)
+                    quant_x(hh + 1, 0)
+                if c == 2 and hh < 5:
+                    quant_x(hh + 1, 1)
+                    if g == 0:
+                        quant_beta(b)
+        quant_v(waiting[0][0], waiting[0][1])
+        last = BATCH - 1
+        stage2(last, 0, 0, nc.scalar.copy)
+        stage2(last, 1, 0, nc.scalar.copy)
+        stage2(last, 0, 1, nc.scalar.copy)
+        stage2(last, 1, 1, nc.vector.tensor_copy)

@@ -29,7 +29,6 @@ def tile_text2imgca_pb_kernel(tc, beta, x2, Wv, bv, out):
         vgp = ctx.enter_context(tc.tile_pool(name="vgp", bufs=4))
         otp = ctx.enter_context(tc.tile_pool(name="otp", bufs=4))
         psum = ctx.enter_context(tc.psum_pool(name="psum", bufs=8))
-        ctx.enter_context(tc.manual_schedule())
 
         def new_bank(name):
             return psum.tile([P, 512], F32, name=name, tag="bank")

@@ -16,7 +16,7 @@ P = 128
 BATCH = 3
 IC = 1024
 TC = 1024
-W_SPLIT = 640
+W_SPLIT = (352, 176)
 
 
 def tile_text2imgca_pb_kernel(tc, beta, x2, Wv, bv, out):
@@ -27,31 +27,30 @@ def tile_text2imgca_pb_kernel(tc, beta, x2, Wv, bv, out):
         xgp = ctx.enter_context(tc.tile_pool(name="xgp", bufs=2))
         xcp = ctx.enter_context(tc.tile_pool(name="xcp", bufs=2))
         vgp = ctx.enter_context(tc.tile_pool(name="vgp", bufs=4))
-        otp = ctx.enter_context(tc.tile_pool(name="otp", bufs=4))
+        otp = ctx.enter_context(tc.tile_pool(name="otp", bufs=8))
         psum = ctx.enter_context(tc.psum_pool(name="psum", bufs=8))
+        ctx.enter_context(tc.manual_schedule())
 
         def new_bank(name):
             return psum.tile([P, 512], F32, name=name, tag="bank")
 
         brow = keep.tile([P, TC], BF16, name="brow")
         nc.vector.memset(brow[:], 0.0)
-        nc.sync.dma_start(out=brow[0:1, :], in_=bv.rearrange("(o c) -> o c", o=1))
         ones = keep.tile([P, P], BF16, name="ones")
         nc.vector.memset(ones[:], 1.0)
         ident = keep.tile([P, P], F32, name="ident")
         make_identity(nc, ident[:])
 
-        wr = []
-        for kg in range(2):
-            t = keep.tile([P, 4, TC], BF16, name="wr%d" % kg)
-            nc.sync.dma_start(
-                out=t[:].rearrange("p (ku ke) c -> p ku (ke c)", ku=2),
-                in_=Wv[512 * kg : 512 * (kg + 1), :].rearrange("(ku q ke) c -> q ku (ke c)", ku=2, ke=2),
-            )
-            wr.append(t)
-
+        wr = [keep.tile([P, 8, 512], BF16, name="wr%d" % hw) for hw in range(2)]
         xr = [keep.tile([P, 4, IC], BF16, name="xr%d" % hh) for hh in range(6)]
         br = [keep.tile([P, 2, 1024], BF16, name="br%d" % b) for b in range(BATCH)]
+        wv_rows = Wv.rearrange("(kk q ke) c -> q kk ke c", kk=4, ke=2)
+
+        def load_w(hw, ke):
+            nc.sync.dma_start(
+                out=wr[hw][:].rearrange("p (kk ke) c -> p kk ke c", ke=2)[:, :, ke, :],
+                in_=wv_rows[:, :, ke, 512 * hw : 512 * (hw + 1)],
+            )
 
         def load_x(hh, pieces):
             b, g = divmod(hh, 2)
@@ -71,7 +70,12 @@ def tile_text2imgca_pb_kernel(tc, beta, x2, Wv, bv, out):
         def load_beta(b):
             nc.sync.dma_start(out=br[b][:], in_=beta[b].rearrange("(nt n) k -> n nt k", nt=2))
 
+        load_w(0, 0)
+        nc.sync.dma_start(out=brow[0:1, :], in_=bv.rearrange("(o c) -> o c", o=1))
+        load_w(0, 1)
         load_x(0, 2)
+        load_w(1, 0)
+        load_w(1, 1)
         load_x(1, 1)
         load_beta(0)
         load_x(2, 1)
@@ -87,29 +91,26 @@ def tile_text2imgca_pb_kernel(tc, beta, x2, Wv, bv, out):
             nc.tensor.matmul(out=pb[:], lhsT=ones[:], rhs=brow[:, 512 * h : 512 * (h + 1)], start=True, stop=True)
             nc.scalar.copy(out=bias[:, 512 * h : 512 * (h + 1)], in_=pb[:])
 
-        wg = [keep.tile([P, TC, 4], BF16, name="wg%d" % kg, align_bytes=64) for kg in range(2)]
-        wc = [keep.tile([P, TC], U32, name="wc%d" % kg, align_bytes=64) for kg in range(2)]
-        ws = [keep.tile([P, TC], U8, name="ws%d" % kg, align_bytes=64) for kg in range(2)]
+        wg = [keep.tile([P, 2, 512, 4], BF16, name="wg%d" % hw, align_bytes=64) for hw in range(2)]
+        wc = [keep.tile([P, 2, 512], U32, name="wc%d" % hw, align_bytes=64) for hw in range(2)]
+        ws = [keep.tile([P, 2, 512], U8, name="ws%d" % hw, align_bytes=64) for hw in range(2)]
 
-        def regroup_w(kg, c0, c1, copy):
+        def regroup_w(hw, kg, c0, c1, copy):
             copy(
-                out=wg[kg][:, c0:c1, :].rearrange("p (c i) t -> p c t i", i=4),
-                in_=wr[kg][:, :, c0:c1].rearrange("p t (c i) -> p c t i", i=4),
+                out=wg[hw][:, kg, c0:c1, :].rearrange("p (c i) t -> p c t i", i=4),
+                in_=wr[hw][:, 4 * kg : 4 * kg + 4, c0:c1].rearrange("p t (c i) -> p c t i", i=4),
             )
 
-        def quant_w(kg, h):
-            cols = slice(512 * h, 512 * (h + 1))
-            nc.vector.quantize_mx(
-                out=wc[kg][:, cols].bitcast(FP8X4),
-                scales=ws[kg][:, cols],
-                in_=wg[kg][:, cols, :].rearrange("p c t -> p (c t)"),
-            )
-
-        for kg in range(2):
-            regroup_w(kg, 0, W_SPLIT, nc.vector.tensor_copy)
-            regroup_w(kg, W_SPLIT, TC, nc.scalar.copy)
-            quant_w(kg, 0)
-            quant_w(kg, 1)
+        def prepare_w(hw):
+            for kg in range(2):
+                regroup_w(hw, kg, 0, W_SPLIT[hw], nc.vector.tensor_copy)
+                regroup_w(hw, kg, W_SPLIT[hw], 512, nc.scalar.copy)
+            for kg in range(2):
+                nc.vector.quantize_mx(
+                    out=wc[hw][:, kg, :].bitcast(FP8X4),
+                    scales=ws[hw][:, kg, :],
+                    in_=wg[hw][:, kg, :, :].rearrange("p c t -> p (c t)"),
+                )
 
         xg = {}
         xc = {}
@@ -174,7 +175,8 @@ def tile_text2imgca_pb_kernel(tc, beta, x2, Wv, bv, out):
 
         def stage1(hh, c):
             bank = new_bank("s1_%d_%d" % (hh, c))
-            cols = slice(128 * c, 128 * (c + 1))
+            hw, q = divmod(c, 4)
+            cols = slice(128 * q, 128 * (q + 1))
             for j in range(4):
                 for kg in range(2):
                     sl = slice(128 * (2 * j + kg), 128 * (2 * j + kg + 1))
@@ -182,8 +184,8 @@ def tile_text2imgca_pb_kernel(tc, beta, x2, Wv, bv, out):
                         out=bank[:, 128 * j : 128 * (j + 1)],
                         lhsT=xc[hh][:, sl].bitcast(FP8X4),
                         lhsT_scale=xs[hh][:, sl],
-                        rhs=wc[kg][:, cols].bitcast(FP8X4),
-                        rhs_scale=ws[kg][:, cols],
+                        rhs=wc[hw][:, kg, cols].bitcast(FP8X4),
+                        rhs_scale=ws[hw][:, kg, cols],
                         start=(kg == 0),
                         stop=(kg == 1),
                     )
@@ -191,7 +193,7 @@ def tile_text2imgca_pb_kernel(tc, beta, x2, Wv, bv, out):
             nc.vector.tensor_tensor(
                 out=vg[(hh, c)][:].rearrange("p (w j) -> p w j", j=4),
                 in0=bank[:].rearrange("p (j w) -> p w j", j=4),
-                in1=bias[:, cols].unsqueeze(2).to_broadcast([P, 128, 4]),
+                in1=bias[:, 128 * c : 128 * (c + 1)].unsqueeze(2).to_broadcast([P, 128, 4]),
                 op=ADD,
             )
 
@@ -203,51 +205,77 @@ def tile_text2imgca_pb_kernel(tc, beta, x2, Wv, bv, out):
                 in_=vg[(hh, c)][:],
             )
 
-        def stage2(b, nt, h, copy):
-            bank = new_bank("s2_%d_%d_%d" % (b, nt, h))
-            for g in range(2):
-                sl = slice(128 * (2 * g + nt), 128 * (2 * g + nt + 1))
-                nc.tensor.matmul_mx(
-                    out=bank[:],
-                    lhsT=bc[b][:, sl].bitcast(FP8X4),
-                    lhsT_scale=bs[b][:, sl],
-                    rhs=vc[(2 * b + g, h)][:].bitcast(FP8X4),
-                    rhs_scale=vs[(2 * b + g, h)][:],
-                    start=(g == 0),
-                    stop=(g == 1),
-                )
-            ot = otp.tile([P, 512], F32, name="ot%d_%d_%d" % (b, nt, h), tag="ot")
-            copy(out=ot[:], in_=bank[:])
-            nc.sync.dma_start(out=out[b, 128 * nt : 128 * (nt + 1), 512 * h : 512 * (h + 1)], in_=ot[:])
+        def stage2_pass(bank, b, nt, g, c0, c1):
+            h = c0 // 4
+            cols = slice(128 * (c0 - 4 * h), 128 * (c1 - 4 * h))
+            sl = slice(128 * (2 * g + nt), 128 * (2 * g + nt + 1))
+            nc.tensor.matmul_mx(
+                out=bank[:, 0 : 128 * (c1 - c0)],
+                lhsT=bc[b][:, sl].bitcast(FP8X4),
+                lhsT_scale=bs[b][:, sl],
+                rhs=vc[(2 * b + g, h)][:, cols].bitcast(FP8X4),
+                rhs_scale=vs[(2 * b + g, h)][:, cols],
+                start=(g == 0),
+                stop=(g == 1),
+            )
 
+        def stage2_out(bank, b, nt, c0, c1, copy):
+            width = 128 * (c1 - c0)
+            ot = otp.tile([P, 512], F32, name="ot%d_%d_%d" % (b, nt, c0), tag="ot")
+            copy(out=ot[:, 0:width], in_=bank[:, 0:width])
+            nc.sync.dma_start(out=out[b, 128 * nt : 128 * (nt + 1), 128 * c0 : 128 * c1], in_=ot[:, 0:width])
+
+        def stage2(b, nt, c0, c1, copy):
+            bank = new_bank("s2_%d_%d_%d" % (b, nt, c0))
+            stage2_pass(bank, b, nt, 0, c0, c1)
+            stage2_pass(bank, b, nt, 1, c0, c1)
+            stage2_out(bank, b, nt, c0, c1, copy)
+
+        prepare_w(0)
         transpose_x(0)
         quant_x(0, 0)
         quant_x(0, 1)
         waiting = []
         for hh in range(6):
             b, g = divmod(hh, 2)
+            t_at = 3 if hh == 0 else 1
             for c in range(8):
                 stage1(hh, c)
                 if waiting:
                     quant_v(waiting[0][0], waiting[0][1])
                 waiting = [(hh, c)]
+                if hh == 0 and c == 1:
+                    prepare_w(1)
                 if g == 0 and b > 0:
-                    if c == 0 or c == 1:
-                        stage2(b - 1, c, 0, nc.scalar.copy)
-                    if c == 3 or c == 4:
-                        stage2(b - 1, c - 3, 1, nc.scalar.copy)
-                if c == 1 and hh < 5:
+                    if c == 0:
+                        stage2(b - 1, 0, 0, 4, nc.scalar.copy)
+                    if c == 2:
+                        stage2(b - 1, 1, 0, 4, nc.scalar.copy)
+                    if c == 3:
+                        stage2(b - 1, 0, 4, 8, nc.scalar.copy)
+                    if c == 4:
+                        stage2(b - 1, 1, 4, 8, nc.scalar.copy)
+                if hh == 5 and c >= 6:
+                    stage2(b, c - 6, 0, 4, nc.scalar.copy)
+                if c == t_at and hh < 5:
                     transpose_x(hh + 1)
                     if g == 0:
                         transpose_beta(b)
                     quant_x(hh + 1, 0)
-                if c == 2 and hh < 5:
+                if c == t_at + 1 and hh < 5:
                     quant_x(hh + 1, 1)
                     if g == 0:
                         quant_beta(b)
         quant_v(waiting[0][0], waiting[0][1])
         last = BATCH - 1
-        stage2(last, 0, 0, nc.scalar.copy)
-        stage2(last, 1, 0, nc.scalar.copy)
-        stage2(last, 0, 1, nc.scalar.copy)
-        stage2(last, 1, 1, nc.vector.tensor_copy)
+        for nt in range(2):
+            stage2(last, nt, 4, 6, nc.scalar.copy)
+        for nt in range(2):
+            stage2(last, nt, 6, 7, nc.scalar.copy)
+        end_banks = [new_bank("s2_end%d" % nt) for nt in range(2)]
+        for nt in range(2):
+            stage2_pass(end_banks[nt], last, nt, 0, 7, 8)
+        for nt in range(2):
+            stage2_pass(end_banks[nt], last, nt, 1, 7, 8)
+        stage2_out(end_banks[0], last, 0, 7, 8, nc.scalar.copy)
+        stage2_out(end_banks[1], last, 1, 7, 8, nc.vector.tensor_copy)

@@ -16,7 +16,7 @@ P = 128
 BATCH = 3
 IC = 1024
 TC = 1024
-W_SPLIT = (352, 176)
+W_SPLIT = (416, 176)
 
 
 def tile_text2imgca_pb_kernel(tc, beta, x2, Wv, bv, out):
@@ -26,7 +26,7 @@ def tile_text2imgca_pb_kernel(tc, beta, x2, Wv, bv, out):
         keep = ctx.enter_context(tc.tile_pool(name="keep", bufs=1))
         xgp = ctx.enter_context(tc.tile_pool(name="xgp", bufs=2))
         xcp = ctx.enter_context(tc.tile_pool(name="xcp", bufs=2))
-        vgp = ctx.enter_context(tc.tile_pool(name="vgp", bufs=4))
+        vgp = ctx.enter_context(tc.tile_pool(name="vgp", bufs=3))
         otp = ctx.enter_context(tc.tile_pool(name="otp", bufs=8))
         psum = ctx.enter_context(tc.psum_pool(name="psum", bufs=8))
         ctx.enter_context(tc.manual_schedule())
@@ -189,20 +189,23 @@ def tile_text2imgca_pb_kernel(tc, beta, x2, Wv, bv, out):
                         start=(kg == 0),
                         stop=(kg == 1),
                     )
-            vg[(hh, c)] = vgp.tile([P, 512], BF16, name="vg%d_%d" % (hh, c), tag="vg", align_bytes=64)
+            if c % 2 == 0:
+                vg[(hh, c // 2)] = vgp.tile([P, 1024], BF16, name="vg%d_%d" % (hh, c), tag="vg", align_bytes=64)
+            half = slice(512 * (c % 2), 512 * (c % 2 + 1))
             nc.vector.tensor_tensor(
-                out=vg[(hh, c)][:].rearrange("p (w j) -> p w j", j=4),
+                out=vg[(hh, c // 2)][:, half].rearrange("p (w j) -> p w j", j=4),
                 in0=bank[:].rearrange("p (j w) -> p w j", j=4),
                 in1=bias[:, 128 * c : 128 * (c + 1)].unsqueeze(2).to_broadcast([P, 128, 4]),
                 op=ADD,
             )
 
-        def quant_v(hh, c):
-            h, q = divmod(c, 4)
+        def quant_v(hh, c0, c1):
+            h = c0 // 4
+            cols = slice(128 * (c0 - 4 * h), 128 * (c1 - 4 * h))
             nc.vector.quantize_mx(
-                out=vc[(hh, h)][:, 128 * q : 128 * (q + 1)].bitcast(FP8X4),
-                scales=vs[(hh, h)][:, 128 * q : 128 * (q + 1)],
-                in_=vg[(hh, c)][:],
+                out=vc[(hh, h)][:, cols].bitcast(FP8X4),
+                scales=vs[(hh, h)][:, cols],
+                in_=vg[(hh, c0 // 2)][:, 512 * (c0 % 2) : 512 * (c0 % 2) + 512 * (c1 - c0)],
             )
 
         def stage2_pass(bank, b, nt, g, c0, c1):
@@ -242,9 +245,13 @@ def tile_text2imgca_pb_kernel(tc, beta, x2, Wv, bv, out):
             for c in range(8):
                 stage1(hh, c)
                 if waiting:
-                    quant_v(waiting[0][0], waiting[0][1])
-                waiting = [(hh, c)]
-                if hh == 0 and c == 1:
+                    quant_v(waiting[0][0], waiting[0][1], waiting[0][2])
+                    waiting = []
+                if c % 2 == 1 and not (hh == 5 and c == 7):
+                    waiting = [(hh, c - 1, c + 1)]
+                if hh == 5 and c == 6:
+                    waiting = [(hh, 6, 7)]
+                if hh == 0 and c == 2:
                     prepare_w(1)
                 if g == 0 and b > 0:
                     if c == 0:
@@ -266,7 +273,7 @@ def tile_text2imgca_pb_kernel(tc, beta, x2, Wv, bv, out):
                     quant_x(hh + 1, 1)
                     if g == 0:
                         quant_beta(b)
-        quant_v(waiting[0][0], waiting[0][1])
+        quant_v(5, 7, 8)
         last = BATCH - 1
         for nt in range(2):
             stage2(last, nt, 4, 6, nc.scalar.copy)

@@ -12,11 +12,12 @@ U8 = mybir.dt.uint8
 FP8X4 = mybir.dt.float8_e4m3fn_x4
 ADD = mybir.AluOpType.add
 
+WARM = (4, 6, 2, 3)
 P = 128
 BATCH = 3
 IC = 1024
 TC = 1024
-W_SPLIT = (416, 176)
+W_SPLIT = (352, 176)
 
 
 def tile_text2imgca_pb_kernel(tc, beta, x2, Wv, bv, out):
@@ -26,7 +27,7 @@ def tile_text2imgca_pb_kernel(tc, beta, x2, Wv, bv, out):
         keep = ctx.enter_context(tc.tile_pool(name="keep", bufs=1))
         xgp = ctx.enter_context(tc.tile_pool(name="xgp", bufs=2))
         xcp = ctx.enter_context(tc.tile_pool(name="xcp", bufs=2))
-        vgp = ctx.enter_context(tc.tile_pool(name="vgp", bufs=3))
+        vgp = ctx.enter_context(tc.tile_pool(name="vgp", bufs=4))
         otp = ctx.enter_context(tc.tile_pool(name="otp", bufs=8))
         psum = ctx.enter_context(tc.psum_pool(name="psum", bufs=8))
         ctx.enter_context(tc.manual_schedule())
@@ -40,6 +41,13 @@ def tile_text2imgca_pb_kernel(tc, beta, x2, Wv, bv, out):
         nc.vector.memset(ones[:], 1.0)
         ident = keep.tile([P, P], F32, name="ident")
         make_identity(nc, ident[:])
+        idle_in = keep.tile([P, 512], BF16, name="idle_in")
+        nc.vector.memset(idle_in[:], 0.0)
+        idle_bank = new_bank("idle_bank")
+
+        def keep_clock_up(count):
+            for i in range(count):
+                nc.tensor.matmul(out=idle_bank[:], lhsT=ones[:], rhs=idle_in[:], start=True, stop=True)
 
         wr = [keep.tile([P, 8, 512], BF16, name="wr%d" % hw) for hw in range(2)]
         xr = [keep.tile([P, 4, IC], BF16, name="xr%d" % hh) for hh in range(6)]
@@ -85,6 +93,7 @@ def tile_text2imgca_pb_kernel(tc, beta, x2, Wv, bv, out):
         load_x(5, 1)
         load_beta(2)
 
+        keep_clock_up(WARM[0])
         bias = keep.tile([P, TC], F32, name="bias")
         for h in range(2):
             pb = new_bank("pb%d" % h)
@@ -134,6 +143,10 @@ def tile_text2imgca_pb_kernel(tc, beta, x2, Wv, bv, out):
                     out=dst[:, 512 * j : 512 * (j + 1)].rearrange("p (kg r ku) -> p kg r ku", kg=2, ku=2),
                     in_=bank[:].rearrange("p (kg ku r) -> p kg r ku", kg=2, ku=2),
                 )
+                if hh == 0 and j == 1:
+                    keep_clock_up(WARM[2])
+                if hh == 0 and j == 3:
+                    keep_clock_up(WARM[3])
 
         def quant_x(hh, part):
             nc.vector.quantize_mx(
@@ -189,23 +202,20 @@ def tile_text2imgca_pb_kernel(tc, beta, x2, Wv, bv, out):
                         start=(kg == 0),
                         stop=(kg == 1),
                     )
-            if c % 2 == 0:
-                vg[(hh, c // 2)] = vgp.tile([P, 1024], BF16, name="vg%d_%d" % (hh, c), tag="vg", align_bytes=64)
-            half = slice(512 * (c % 2), 512 * (c % 2 + 1))
+            vg[(hh, c)] = vgp.tile([P, 512], BF16, name="vg%d_%d" % (hh, c), tag="vg", align_bytes=64)
             nc.vector.tensor_tensor(
-                out=vg[(hh, c // 2)][:, half].rearrange("p (w j) -> p w j", j=4),
+                out=vg[(hh, c)][:].rearrange("p (w j) -> p w j", j=4),
                 in0=bank[:].rearrange("p (j w) -> p w j", j=4),
                 in1=bias[:, 128 * c : 128 * (c + 1)].unsqueeze(2).to_broadcast([P, 128, 4]),
                 op=ADD,
             )
 
-        def quant_v(hh, c0, c1):
-            h = c0 // 4
-            cols = slice(128 * (c0 - 4 * h), 128 * (c1 - 4 * h))
+        def quant_v(hh, c):
+            h, q = divmod(c, 4)
             nc.vector.quantize_mx(
-                out=vc[(hh, h)][:, cols].bitcast(FP8X4),
-                scales=vs[(hh, h)][:, cols],
-                in_=vg[(hh, c0 // 2)][:, 512 * (c0 % 2) : 512 * (c0 % 2) + 512 * (c1 - c0)],
+                out=vc[(hh, h)][:, 128 * q : 128 * (q + 1)].bitcast(FP8X4),
+                scales=vs[(hh, h)][:, 128 * q : 128 * (q + 1)],
+                in_=vg[(hh, c)][:],
             )
 
         def stage2_pass(bank, b, nt, g, c0, c1):
@@ -235,6 +245,7 @@ def tile_text2imgca_pb_kernel(tc, beta, x2, Wv, bv, out):
             stage2_out(bank, b, nt, c0, c1, copy)
 
         prepare_w(0)
+        keep_clock_up(WARM[1])
         transpose_x(0)
         quant_x(0, 0)
         quant_x(0, 1)
@@ -245,13 +256,9 @@ def tile_text2imgca_pb_kernel(tc, beta, x2, Wv, bv, out):
             for c in range(8):
                 stage1(hh, c)
                 if waiting:
-                    quant_v(waiting[0][0], waiting[0][1], waiting[0][2])
-                    waiting = []
-                if c % 2 == 1 and not (hh == 5 and c == 7):
-                    waiting = [(hh, c - 1, c + 1)]
-                if hh == 5 and c == 6:
-                    waiting = [(hh, 6, 7)]
-                if hh == 0 and c == 2:
+                    quant_v(waiting[0][0], waiting[0][1])
+                waiting = [(hh, c)]
+                if hh == 0 and c == 1:
                     prepare_w(1)
                 if g == 0 and b > 0:
                     if c == 0:
@@ -273,7 +280,7 @@ def tile_text2imgca_pb_kernel(tc, beta, x2, Wv, bv, out):
                     quant_x(hh + 1, 1)
                     if g == 0:
                         quant_beta(b)
-        quant_v(5, 7, 8)
+        quant_v(waiting[0][0], waiting[0][1])
         last = BATCH - 1
         for nt in range(2):
             stage2(last, nt, 4, 6, nc.scalar.copy)

@@ -54,10 +54,10 @@ def tile_text2imgca_pb_kernel(tc, beta, x2, Wv, bv, out):
         br = [keep.tile([P, 2, 1024], BF16, name="br%d" % b) for b in range(BATCH)]
         wv_rows = Wv.rearrange("(kk q ke) c -> q kk ke c", kk=4, ke=2)
 
-        def load_w(hw, ke):
+        def load_w(hw, kk):
             nc.sync.dma_start(
-                out=wr[hw][:].rearrange("p (kk ke) c -> p kk ke c", ke=2)[:, :, ke, :],
-                in_=wv_rows[:, :, ke, 512 * hw : 512 * (hw + 1)],
+                out=wr[hw][:, 2 * kk : 2 * kk + 2, :],
+                in_=wv_rows[:, kk, :, 512 * hw : 512 * (hw + 1)],
             )
 
         def load_x(hh, pieces):
@@ -80,10 +80,11 @@ def tile_text2imgca_pb_kernel(tc, beta, x2, Wv, bv, out):
 
         load_w(0, 0)
         nc.sync.dma_start(out=brow[0:1, :], in_=bv.rearrange("(o c) -> o c", o=1))
-        load_w(0, 1)
+        for kk in range(1, 4):
+            load_w(0, kk)
         load_x(0, 2)
-        load_w(1, 0)
-        load_w(1, 1)
+        for kk in range(4):
+            load_w(1, kk)
         load_x(1, 1)
         load_beta(0)
         load_x(2, 1)
@@ -148,11 +149,13 @@ def tile_text2imgca_pb_kernel(tc, beta, x2, Wv, bv, out):
                 if hh == 0 and j == 3:
                     keep_clock_up(WARM[3])
 
-        def quant_x(hh, part):
+        def quant_x(hh, part, parts=2):
+            width = 1024 // parts
+            cols = slice(width * part, width * (part + 1))
             nc.vector.quantize_mx(
-                out=xc[hh][:, 512 * part : 512 * (part + 1)].bitcast(FP8X4),
-                scales=xs[hh][:, 512 * part : 512 * (part + 1)],
-                in_=xg[hh][:, 2048 * part : 2048 * (part + 1)],
+                out=xc[hh][:, cols].bitcast(FP8X4),
+                scales=xs[hh][:, cols],
+                in_=xg[hh][:, 4 * width * part : 4 * width * (part + 1)],
             )
 
         bg = [keep.tile([P, 2048], BF16, name="bg%d" % b, align_bytes=64) for b in range(BATCH)]
@@ -247,8 +250,8 @@ def tile_text2imgca_pb_kernel(tc, beta, x2, Wv, bv, out):
         prepare_w(0)
         keep_clock_up(WARM[1])
         transpose_x(0)
-        quant_x(0, 0)
-        quant_x(0, 1)
+        for j in range(4):
+            quant_x(0, j, parts=4)
         waiting = []
         for hh in range(6):
             b, g = divmod(hh, 2)

@@ -126,13 +126,12 @@ def tile_text2imgca_pb_kernel(tc, beta, x2, Wv, bv, out):
         xc = {}
         xs = {}
 
-        def transpose_x(hh):
-            xg[hh] = xgp.tile([P, 4096], BF16, name="xg%d" % hh, tag="xg", align_bytes=64)
-            xc[hh] = xcp.tile([P, 1024], U32, name="xc%d" % hh, tag="xc", align_bytes=64)
-            xs[hh] = xcp.tile([P, 1024], U8, name="xs%d" % hh, tag="xs", align_bytes=64)
+        def transpose_x(hh, js):
+            if js[0] == 0:
+                make_x(hh)
             src = xr[hh][:].bitcast(F32)
             dst = xg[hh][:].bitcast(F32)
-            for j in range(4):
+            for j in js:
                 bank = new_bank("xt%d_%d" % (hh, j))
                 for s in range(4):
                     nc.tensor.transpose(
@@ -148,6 +147,11 @@ def tile_text2imgca_pb_kernel(tc, beta, x2, Wv, bv, out):
                     keep_clock_up(WARM[2])
                 if hh == 0 and j == 3:
                     keep_clock_up(WARM[3])
+
+        def make_x(hh):
+            xg[hh] = xgp.tile([P, 4096], BF16, name="xg%d" % hh, tag="xg", align_bytes=64)
+            xc[hh] = xcp.tile([P, 1024], U32, name="xc%d" % hh, tag="xc", align_bytes=64)
+            xs[hh] = xcp.tile([P, 1024], U8, name="xs%d" % hh, tag="xs", align_bytes=64)
 
         def quant_x(hh, part, parts=2):
             width = 1024 // parts
@@ -249,7 +253,7 @@ def tile_text2imgca_pb_kernel(tc, beta, x2, Wv, bv, out):
 
         prepare_w(0)
         keep_clock_up(WARM[1])
-        transpose_x(0)
+        transpose_x(0, (0, 1, 2, 3))
         for j in range(4):
             quant_x(0, j, parts=4)
         waiting = []
@@ -274,15 +278,17 @@ def tile_text2imgca_pb_kernel(tc, beta, x2, Wv, bv, out):
                         stage2(b - 1, 1, 4, 8, nc.scalar.copy)
                 if hh == 5 and c >= 6:
                     stage2(b, c - 6, 0, 4, nc.scalar.copy)
-                if c == t_at and hh < 5:
-                    transpose_x(hh + 1)
+                if hh < 5 and c == t_at:
+                    transpose_x(hh + 1, (0, 1))
+                if hh < 5 and c == t_at + 1:
+                    transpose_x(hh + 1, (2, 3))
+                    quant_x(hh + 1, 0)
+                if hh < 5 and c == t_at + 2:
                     if g == 0:
                         transpose_beta(b)
-                    quant_x(hh + 1, 0)
-                if c == t_at + 1 and hh < 5:
                     quant_x(hh + 1, 1)
-                    if g == 0:
-                        quant_beta(b)
+                if hh < 5 and c == t_at + 3 and g == 0:
+                    quant_beta(b)
         quant_v(waiting[0][0], waiting[0][1])
         last = BATCH - 1
         for nt in range(2):

@@ -12,12 +12,12 @@ U8 = mybir.dt.uint8
 FP8X4 = mybir.dt.float8_e4m3fn_x4
 ADD = mybir.AluOpType.add
 
-WARM = (4, 6, 2, 3)
+WARM = (4, 6, 2, 0)
 P = 128
 BATCH = 3
 IC = 1024
 TC = 1024
-W_SPLIT = (352, 176)
+W_SPLIT = (352, 128)
 
 
 def tile_text2imgca_pb_kernel(tc, beta, x2, Wv, bv, out):
@@ -85,14 +85,13 @@ def tile_text2imgca_pb_kernel(tc, beta, x2, Wv, bv, out):
         load_x(0, 2)
         for kk in range(4):
             load_w(1, kk)
-        load_x(1, 1)
-        load_beta(0)
-        load_x(2, 1)
-        load_x(3, 1)
-        load_beta(1)
-        load_x(4, 1)
-        load_x(5, 1)
-        load_beta(2)
+        load_x(1, 2)
+        for b in range(BATCH):
+            if b + 1 < BATCH:
+                load_x(2 * b + 2, 1)
+            load_beta(b)
+            if b + 1 < BATCH:
+                load_x(2 * b + 3, 1)
 
         keep_clock_up(WARM[0])
         bias = keep.tile([P, TC], F32, name="bias")
@@ -185,6 +184,7 @@ def tile_text2imgca_pb_kernel(tc, beta, x2, Wv, bv, out):
         def quant_beta(b):
             nc.vector.quantize_mx(out=bc[b][:].bitcast(FP8X4), scales=bs[b][:], in_=bg[b][:])
 
+        begun = {}
         vg = {}
         vc = {}
         vs = {}
@@ -193,22 +193,28 @@ def tile_text2imgca_pb_kernel(tc, beta, x2, Wv, bv, out):
                 vc[(hh, h)] = keep.tile([P, 512], U32, name="vc%d_%d" % (hh, h), align_bytes=64)
                 vs[(hh, h)] = keep.tile([P, 512], U8, name="vs%d_%d" % (hh, h), align_bytes=64)
 
-        def stage1(hh, c):
-            bank = new_bank("s1_%d_%d" % (hh, c))
+        def multiply(bank, hh, c, j):
             hw, q = divmod(c, 4)
             cols = slice(128 * q, 128 * (q + 1))
-            for j in range(4):
-                for kg in range(2):
-                    sl = slice(128 * (2 * j + kg), 128 * (2 * j + kg + 1))
-                    nc.tensor.matmul_mx(
-                        out=bank[:, 128 * j : 128 * (j + 1)],
-                        lhsT=xc[hh][:, sl].bitcast(FP8X4),
-                        lhsT_scale=xs[hh][:, sl],
-                        rhs=wc[hw][:, kg, cols].bitcast(FP8X4),
-                        rhs_scale=ws[hw][:, kg, cols],
-                        start=(kg == 0),
-                        stop=(kg == 1),
-                    )
+            for kg in range(2):
+                sl = slice(128 * (2 * j + kg), 128 * (2 * j + kg + 1))
+                nc.tensor.matmul_mx(
+                    out=bank[:, 128 * j : 128 * (j + 1)],
+                    lhsT=xc[hh][:, sl].bitcast(FP8X4),
+                    lhsT_scale=xs[hh][:, sl],
+                    rhs=wc[hw][:, kg, cols].bitcast(FP8X4),
+                    rhs_scale=ws[hw][:, kg, cols],
+                    start=(kg == 0),
+                    stop=(kg == 1),
+                )
+
+        def stage1(hh, c):
+            if (hh, c) in begun:
+                bank = begun[(hh, c)]
+            else:
+                bank = new_bank("s1_%d_%d" % (hh, c))
+                for j in range(4):
+                    multiply(bank, hh, c, j)
             vg[(hh, c)] = vgp.tile([P, 512], BF16, name="vg%d_%d" % (hh, c), tag="vg", align_bytes=64)
             nc.vector.tensor_tensor(
                 out=vg[(hh, c)][:].rearrange("p (w j) -> p w j", j=4),
@@ -256,6 +262,11 @@ def tile_text2imgca_pb_kernel(tc, beta, x2, Wv, bv, out):
         transpose_x(0, (0, 1, 2, 3))
         for j in range(4):
             quant_x(0, j, parts=4)
+        for c in range(3):
+            begun[(0, c)] = new_bank("s1_0_%d" % c)
+        for j in range(4):
+            for c in range(3):
+                multiply(begun[(0, c)], 0, c, j)
         waiting = []
         for hh in range(6):
             b, g = divmod(hh, 2)
@@ -278,16 +289,22 @@ def tile_text2imgca_pb_kernel(tc, beta, x2, Wv, bv, out):
                         stage2(b - 1, 1, 4, 8, nc.scalar.copy)
                 if hh == 5 and c >= 6:
                     stage2(b, c - 6, 0, 4, nc.scalar.copy)
-                if hh < 5 and c == t_at:
-                    transpose_x(hh + 1, (0, 1))
-                if hh < 5 and c == t_at + 1:
-                    transpose_x(hh + 1, (2, 3))
-                    quant_x(hh + 1, 0)
-                if hh < 5 and c == t_at + 2:
-                    if g == 0:
-                        transpose_beta(b)
-                    quant_x(hh + 1, 1)
-                if hh < 5 and c == t_at + 3 and g == 0:
+                if hh == 0 and c == 3:
+                    transpose_x(1, (0, 1, 2, 3))
+                    quant_x(1, 0)
+                if hh == 0 and c == 4:
+                    quant_x(1, 1)
+                if 0 < hh < 5:
+                    if c == 1:
+                        transpose_x(hh + 1, (0, 1))
+                    if c == 2:
+                        transpose_x(hh + 1, (2, 3))
+                        quant_x(hh + 1, 0)
+                    if c == 3:
+                        quant_x(hh + 1, 1)
+                if g == 1 and c == 1:
+                    transpose_beta(b)
+                if g == 1 and c == 3:
                     quant_beta(b)
         quant_v(waiting[0][0], waiting[0][1])
         last = BATCH - 1

@@ -17,6 +17,7 @@ P = 128
 BATCH = 3
 IC = 1024
 TC = 1024
+GPSIMD_C = ((), (0, 4), (0, 4), (0, 4), (0, 4), (0,))
 W_SPLIT = (352, 128)
 
 
@@ -27,7 +28,8 @@ def tile_text2imgca_pb_kernel(tc, beta, x2, Wv, bv, out):
         keep = ctx.enter_context(tc.tile_pool(name="keep", bufs=1))
         xgp = ctx.enter_context(tc.tile_pool(name="xgp", bufs=2))
         xcp = ctx.enter_context(tc.tile_pool(name="xcp", bufs=2))
-        vgp = ctx.enter_context(tc.tile_pool(name="vgp", bufs=4))
+        vgp = ctx.enter_context(tc.tile_pool(name="vgp", bufs=6))
+        yp = ctx.enter_context(tc.tile_pool(name="yp", bufs=1))
         otp = ctx.enter_context(tc.tile_pool(name="otp", bufs=8))
         psum = ctx.enter_context(tc.psum_pool(name="psum", bufs=8))
         ctx.enter_context(tc.manual_schedule())
@@ -215,13 +217,22 @@ def tile_text2imgca_pb_kernel(tc, beta, x2, Wv, bv, out):
                 bank = new_bank("s1_%d_%d" % (hh, c))
                 for j in range(4):
                     multiply(bank, hh, c, j)
-            vg[(hh, c)] = vgp.tile([P, 512], BF16, name="vg%d_%d" % (hh, c), tag="vg", align_bytes=64)
-            nc.vector.tensor_tensor(
-                out=vg[(hh, c)][:].rearrange("p (w j) -> p w j", j=4),
-                in0=bank[:].rearrange("p (j w) -> p w j", j=4),
-                in1=bias[:, 128 * c : 128 * (c + 1)].unsqueeze(2).to_broadcast([P, 128, 4]),
-                op=ADD,
-            )
+            on_gpsimd = c in GPSIMD_C[hh]
+            product = bank[:].rearrange("p (j w) -> p w j", j=4)
+            bias_cols = bias[:, 128 * c : 128 * (c + 1)].unsqueeze(2).to_broadcast([P, 128, 4])
+            if on_gpsimd:
+                y = yp.tile([P, 512], F32, name="y%d_%d" % (hh, c), tag="y")
+                vg[(hh, c)] = yp.tile([P, 512], BF16, name="vg%d_%d" % (hh, c), tag="vg_gpsimd", align_bytes=64)
+                y_grouped = y[:].rearrange("p (w j) -> p w j", j=4)
+                nc.scalar.copy(out=y_grouped, in_=product)
+                nc.gpsimd.tensor_tensor(
+                    out=vg[(hh, c)][:].rearrange("p (w j) -> p w j", j=4), in0=y_grouped, in1=bias_cols, op=ADD
+                )
+            else:
+                vg[(hh, c)] = vgp.tile([P, 512], BF16, name="vg%d_%d" % (hh, c), tag="vg", align_bytes=64)
+                nc.vector.tensor_tensor(
+                    out=vg[(hh, c)][:].rearrange("p (w j) -> p w j", j=4), in0=product, in1=bias_cols, op=ADD
+                )
 
         def quant_v(hh, c):
             h, q = divmod(c, 4)
@@ -267,15 +278,10 @@ def tile_text2imgca_pb_kernel(tc, beta, x2, Wv, bv, out):
         for j in range(4):
             for c in range(3):
                 multiply(begun[(0, c)], 0, c, j)
-        waiting = []
         for hh in range(6):
             b, g = divmod(hh, 2)
-            t_at = 3 if hh == 0 else 1
             for c in range(8):
                 stage1(hh, c)
-                if waiting:
-                    quant_v(waiting[0][0], waiting[0][1])
-                waiting = [(hh, c)]
                 if hh == 0 and c == 1:
                     prepare_w(1)
                 if g == 0 and b > 0:
@@ -291,22 +297,29 @@ def tile_text2imgca_pb_kernel(tc, beta, x2, Wv, bv, out):
                     stage2(b, c - 6, 0, 4, nc.scalar.copy)
                 if hh == 0 and c == 3:
                     transpose_x(1, (0, 1, 2, 3))
-                    quant_x(1, 0)
-                if hh == 0 and c == 4:
-                    quant_x(1, 1)
                 if 0 < hh < 5:
-                    if c == 1:
+                    if c == 0:
                         transpose_x(hh + 1, (0, 1))
-                    if c == 2:
+                    if c == 1:
                         transpose_x(hh + 1, (2, 3))
-                        quant_x(hh + 1, 0)
-                    if c == 3:
-                        quant_x(hh + 1, 1)
-                if g == 1 and c == 1:
+                if g == 1 and c == 2:
                     transpose_beta(b)
+                if hh == 0 and c in (3, 4):
+                    quant_x(1, c - 3)
+                if 0 < hh < 5 and c == 3:
+                    quant_x(hh + 1, 0)
+                    quant_x(hh + 1, 1)
                 if g == 1 and c == 3:
                     quant_beta(b)
-        quant_v(waiting[0][0], waiting[0][1])
+                if any(q in GPSIMD_C[hh] for q in range(c - c % 4, c + 1)):
+                    if c % 4 == 3:
+                        for q in (c - 2, c - 1, c, c - 3):
+                            quant_v(hh, q)
+                else:
+                    if c % 4 > 0 or (hh, c) == (0, 4):
+                        quant_v(hh, c - 1)
+                    if c % 4 == 3 and (hh, c) != (0, 3):
+                        quant_v(hh, c)
         last = BATCH - 1
         for nt in range(2):
             stage2(last, nt, 4, 6, nc.scalar.copy)

@@ -12,7 +12,7 @@ U8 = mybir.dt.uint8
 FP8X4 = mybir.dt.float8_e4m3fn_x4
 ADD = mybir.AluOpType.add
 
-WARM = (4, 6, 2, 0)
+WARM = (4, 6, 2, 2)
 P = 128
 BATCH = 3
 IC = 1024
@@ -146,8 +146,6 @@ def tile_text2imgca_pb_kernel(tc, beta, x2, Wv, bv, out):
                 )
                 if hh == 0 and j == 1:
                     keep_clock_up(WARM[2])
-                if hh == 0 and j == 3:
-                    keep_clock_up(WARM[3])
 
         def make_x(hh):
             xg[hh] = xgp.tile([P, 4096], BF16, name="xg%d" % hh, tag="xg", align_bytes=64)
@@ -167,10 +165,10 @@ def tile_text2imgca_pb_kernel(tc, beta, x2, Wv, bv, out):
         bc = [keep.tile([P, 512], U32, name="bc%d" % b, align_bytes=64) for b in range(BATCH)]
         bs = [keep.tile([P, 512], U8, name="bs%d" % b, align_bytes=64) for b in range(BATCH)]
 
-        def transpose_beta(b):
+        def transpose_beta(b, nts):
             src = br[b][:].bitcast(F32)
             dst = bg[b][:].bitcast(F32).rearrange("p (g nt n u) -> p g nt n u", g=2, nt=2, u=2)
-            for nt in range(2):
+            for nt in nts:
                 bank = new_bank("bt%d_%d" % (b, nt))
                 for s in range(4):
                     nc.tensor.transpose(
@@ -285,31 +283,33 @@ def tile_text2imgca_pb_kernel(tc, beta, x2, Wv, bv, out):
                 if hh == 0 and c == 1:
                     prepare_w(1)
                 if g == 0 and b > 0:
-                    if c == 0:
-                        stage2(b - 1, 0, 0, 4, nc.scalar.copy)
-                    if c == 2:
-                        stage2(b - 1, 1, 0, 4, nc.scalar.copy)
                     if c == 3:
-                        stage2(b - 1, 0, 4, 8, nc.scalar.copy)
+                        stage2(b - 1, 0, 0, 4, nc.scalar.copy)
                     if c == 4:
+                        stage2(b - 1, 1, 0, 4, nc.scalar.copy)
+                    if c == 5:
+                        stage2(b - 1, 0, 4, 8, nc.scalar.copy)
+                    if c == 6:
                         stage2(b - 1, 1, 4, 8, nc.scalar.copy)
                 if hh == 5 and c >= 6:
                     stage2(b, c - 6, 0, 4, nc.scalar.copy)
                 if hh == 0 and c == 3:
-                    transpose_x(1, (0, 1, 2, 3))
-                if 0 < hh < 5:
-                    if c == 0:
-                        transpose_x(hh + 1, (0, 1))
-                    if c == 1:
-                        transpose_x(hh + 1, (2, 3))
-                if g == 1 and c == 2:
-                    transpose_beta(b)
+                    transpose_x(1, (0, 1))
+                    keep_clock_up(WARM[3])
+                    transpose_x(1, (2, 3))
+                if c in (0, 2):
+                    if 0 < hh < 5:
+                        transpose_x(hh + 1, (c, c + 1))
+                    if hh in (1, 3):
+                        transpose_beta(b, (c // 2,))
+                if hh == 5 and c == 0:
+                    transpose_beta(b, (0, 1))
                 if hh == 0 and c in (3, 4):
                     quant_x(1, c - 3)
                 if 0 < hh < 5 and c == 3:
                     quant_x(hh + 1, 0)
                     quant_x(hh + 1, 1)
-                if g == 1 and c == 3:
+                if hh in (1, 3) and c == 7 or hh == 5 and c == 3:
                     quant_beta(b)
                 if any(q in GPSIMD_C[hh] for q in range(c - c % 4, c + 1)):
                     if c % 4 == 3:

@@ -17,6 +17,7 @@ P = 128
 BATCH = 3
 IC = 1024
 TC = 1024
+BETA_AT = {1: 0, 3: 1, 4: 2}
 GPSIMD_C = ((), (0, 4), (0, 4), (0, 4), (0, 4), (0,))
 W_SPLIT = (352, 128)
 
@@ -28,7 +29,7 @@ def tile_text2imgca_pb_kernel(tc, beta, x2, Wv, bv, out):
         keep = ctx.enter_context(tc.tile_pool(name="keep", bufs=1))
         xgp = ctx.enter_context(tc.tile_pool(name="xgp", bufs=2))
         xcp = ctx.enter_context(tc.tile_pool(name="xcp", bufs=2))
-        vgp = ctx.enter_context(tc.tile_pool(name="vgp", bufs=6))
+        vgp = ctx.enter_context(tc.tile_pool(name="vgp", bufs=14))
         yp = ctx.enter_context(tc.tile_pool(name="yp", bufs=1))
         otp = ctx.enter_context(tc.tile_pool(name="otp", bufs=8))
         psum = ctx.enter_context(tc.psum_pool(name="psum", bufs=8))
@@ -300,25 +301,29 @@ def tile_text2imgca_pb_kernel(tc, beta, x2, Wv, bv, out):
                 if c in (0, 2):
                     if 0 < hh < 5:
                         transpose_x(hh + 1, (c, c + 1))
-                    if hh in (1, 3):
-                        transpose_beta(b, (c // 2,))
-                if hh == 5 and c == 0:
-                    transpose_beta(b, (0, 1))
+                    if hh in BETA_AT:
+                        transpose_beta(BETA_AT[hh], (c // 2,))
                 if hh == 0 and c in (3, 4):
                     quant_x(1, c - 3)
                 if 0 < hh < 5 and c == 3:
                     quant_x(hh + 1, 0)
                     quant_x(hh + 1, 1)
-                if hh in (1, 3) and c == 7 or hh == 5 and c == 3:
-                    quant_beta(b)
+                if hh in BETA_AT and c == 7:
+                    quant_beta(BETA_AT[hh])
+                if (hh, c) == (1, 3):
+                    for q in range(4):
+                        quant_v(0, q)
+                if (hh, c) == (1, 7):
+                    for q in range(4, 8):
+                        quant_v(0, q)
                 if any(q in GPSIMD_C[hh] for q in range(c - c % 4, c + 1)):
                     if c % 4 == 3:
                         for q in (c - 2, c - 1, c, c - 3):
                             quant_v(hh, q)
-                else:
-                    if c % 4 > 0 or (hh, c) == (0, 4):
+                elif hh > 0:
+                    if c % 4 > 0:
                         quant_v(hh, c - 1)
-                    if c % 4 == 3 and (hh, c) != (0, 3):
+                    if c % 4 == 3:
                         quant_v(hh, c)
         last = BATCH - 1
         for nt in range(2):

@@ -12,14 +12,17 @@ U8 = mybir.dt.uint8
 FP8X4 = mybir.dt.float8_e4m3fn_x4
 ADD = mybir.AluOpType.add
 
-WARM = (4, 6, 2, 2)
 P = 128
 BATCH = 3
+HALVES = 2 * BATCH
 IC = 1024
 TC = 1024
-BETA_AT = {1: 0, 3: 1, 4: 2}
-GPSIMD_C = ((), (0, 4), (0, 4), (0, 4), (0, 4), (0,))
+
 W_SPLIT = (352, 128)
+
+WARM_BIAS, WARM_X, WARM_BETWEEN = 4, 6, 2
+
+HEAD_GROUPS = 3
 
 
 def tile_text2imgca_pb_kernel(tc, beta, x2, Wv, bv, out):
@@ -30,7 +33,7 @@ def tile_text2imgca_pb_kernel(tc, beta, x2, Wv, bv, out):
         xgp = ctx.enter_context(tc.tile_pool(name="xgp", bufs=2))
         xcp = ctx.enter_context(tc.tile_pool(name="xcp", bufs=2))
         vgp = ctx.enter_context(tc.tile_pool(name="vgp", bufs=14))
-        yp = ctx.enter_context(tc.tile_pool(name="yp", bufs=1))
+        gpsimd_pool = ctx.enter_context(tc.tile_pool(name="gpsimd_pool", bufs=1))
         otp = ctx.enter_context(tc.tile_pool(name="otp", bufs=8))
         psum = ctx.enter_context(tc.psum_pool(name="psum", bufs=8))
         ctx.enter_context(tc.manual_schedule())
@@ -53,8 +56,8 @@ def tile_text2imgca_pb_kernel(tc, beta, x2, Wv, bv, out):
                 nc.tensor.matmul(out=idle_bank[:], lhsT=ones[:], rhs=idle_in[:], start=True, stop=True)
 
         wr = [keep.tile([P, 8, 512], BF16, name="wr%d" % hw) for hw in range(2)]
-        xr = [keep.tile([P, 4, IC], BF16, name="xr%d" % hh) for hh in range(6)]
-        br = [keep.tile([P, 2, 1024], BF16, name="br%d" % b) for b in range(BATCH)]
+        xr = [keep.tile([P, 4, IC], BF16, name="xr%d" % hh) for hh in range(HALVES)]
+        br = [keep.tile([P, 2, 16, 64], BF16, name="br%d" % b, align_bytes=64) for b in range(BATCH)]
         wv_rows = Wv.rearrange("(kk q ke) c -> q kk ke c", kk=4, ke=2)
 
         def load_w(hw, kk):
@@ -79,7 +82,14 @@ def tile_text2imgca_pb_kernel(tc, beta, x2, Wv, bv, out):
                 )
 
         def load_beta(b):
-            nc.sync.dma_start(out=br[b][:], in_=beta[b].rearrange("(nt n) k -> n nt k", nt=2))
+            for g in range(2):
+                for u in range(2):
+                    for q in range(4):
+                        k0 = 512 * g + 256 * u + 64 * q
+                        nc.sync.dma_start(
+                            out=br[b][32 * q + u : 32 * (q + 1) : 2, g, :, :],
+                            in_=beta[b, :, k0 : k0 + 64].rearrange("(nh nl) k -> nl nh k", nl=16),
+                        )
 
         load_w(0, 0)
         nc.sync.dma_start(out=brow[0:1, :], in_=bv.rearrange("(o c) -> o c", o=1))
@@ -89,14 +99,15 @@ def tile_text2imgca_pb_kernel(tc, beta, x2, Wv, bv, out):
         for kk in range(4):
             load_w(1, kk)
         load_x(1, 2)
-        for b in range(BATCH):
-            if b + 1 < BATCH:
-                load_x(2 * b + 2, 1)
-            load_beta(b)
-            if b + 1 < BATCH:
-                load_x(2 * b + 3, 1)
+        load_x(2, 1)
+        load_x(3, 1)
+        load_beta(0)
+        load_x(4, 1)
+        load_beta(1)
+        load_x(5, 1)
+        load_beta(2)
 
-        keep_clock_up(WARM[0])
+        keep_clock_up(WARM_BIAS)
         bias = keep.tile([P, TC], F32, name="bias")
         for h in range(2):
             pb = new_bank("pb%d" % h)
@@ -128,9 +139,12 @@ def tile_text2imgca_pb_kernel(tc, beta, x2, Wv, bv, out):
         xc = {}
         xs = {}
 
+        def new_x(hh):
+            xg[hh] = xgp.tile([P, 4096], BF16, name="xg%d" % hh, tag="xg", align_bytes=64)
+            xc[hh] = xcp.tile([P, 1024], U32, name="xc%d" % hh, tag="xc", align_bytes=64)
+            xs[hh] = xcp.tile([P, 1024], U8, name="xs%d" % hh, tag="xs", align_bytes=64)
+
         def transpose_x(hh, js):
-            if js[0] == 0:
-                make_x(hh)
             src = xr[hh][:].bitcast(F32)
             dst = xg[hh][:].bitcast(F32)
             for j in js:
@@ -145,15 +159,8 @@ def tile_text2imgca_pb_kernel(tc, beta, x2, Wv, bv, out):
                     out=dst[:, 512 * j : 512 * (j + 1)].rearrange("p (kg r ku) -> p kg r ku", kg=2, ku=2),
                     in_=bank[:].rearrange("p (kg ku r) -> p kg r ku", kg=2, ku=2),
                 )
-                if hh == 0 and j == 1:
-                    keep_clock_up(WARM[2])
 
-        def make_x(hh):
-            xg[hh] = xgp.tile([P, 4096], BF16, name="xg%d" % hh, tag="xg", align_bytes=64)
-            xc[hh] = xcp.tile([P, 1024], U32, name="xc%d" % hh, tag="xc", align_bytes=64)
-            xs[hh] = xcp.tile([P, 1024], U8, name="xs%d" % hh, tag="xs", align_bytes=64)
-
-        def quant_x(hh, part, parts=2):
+        def quant_x(hh, part, parts):
             width = 1024 // parts
             cols = slice(width * part, width * (part + 1))
             nc.vector.quantize_mx(
@@ -166,72 +173,56 @@ def tile_text2imgca_pb_kernel(tc, beta, x2, Wv, bv, out):
         bc = [keep.tile([P, 512], U32, name="bc%d" % b, align_bytes=64) for b in range(BATCH)]
         bs = [keep.tile([P, 512], U8, name="bs%d" % b, align_bytes=64) for b in range(BATCH)]
 
-        def transpose_beta(b, nts):
-            src = br[b][:].bitcast(F32)
-            dst = bg[b][:].bitcast(F32).rearrange("p (g nt n u) -> p g nt n u", g=2, nt=2, u=2)
-            for nt in nts:
-                bank = new_bank("bt%d_%d" % (b, nt))
-                for s in range(4):
-                    nc.tensor.transpose(
-                        out=bank[:, 128 * s : 128 * (s + 1)],
-                        in_=src[:, nt, 128 * s : 128 * (s + 1)],
-                        identity=ident[:],
-                    )
-                nc.scalar.copy(
-                    out=dst[:, :, nt, :, :],
-                    in_=bank[:].rearrange("p (g u n) -> p g n u", g=2, u=2),
-                )
+        def turn_beta(b, g):
+            nc.vector.transpose(
+                out=bg[b][:].bitcast(F32)[:, 512 * g : 512 * (g + 1)],
+                in_=br[b][:].rearrange("p g nh k -> p (g nh k)").bitcast(F32)[:, 512 * g : 512 * (g + 1)],
+            )
 
         def quant_beta(b):
             nc.vector.quantize_mx(out=bc[b][:].bitcast(FP8X4), scales=bs[b][:], in_=bg[b][:])
 
-        begun = {}
+        banks = {}
         vg = {}
         vc = {}
         vs = {}
-        for hh in range(6):
+        for hh in range(HALVES):
             for h in range(2):
                 vc[(hh, h)] = keep.tile([P, 512], U32, name="vc%d_%d" % (hh, h), align_bytes=64)
                 vs[(hh, h)] = keep.tile([P, 512], U8, name="vs%d_%d" % (hh, h), align_bytes=64)
 
-        def multiply(bank, hh, c, j):
+        def multiply(hh, c, j):
             hw, q = divmod(c, 4)
             cols = slice(128 * q, 128 * (q + 1))
             for kg in range(2):
-                sl = slice(128 * (2 * j + kg), 128 * (2 * j + kg + 1))
+                pixels = slice(128 * (2 * j + kg), 128 * (2 * j + kg + 1))
                 nc.tensor.matmul_mx(
-                    out=bank[:, 128 * j : 128 * (j + 1)],
-                    lhsT=xc[hh][:, sl].bitcast(FP8X4),
-                    lhsT_scale=xs[hh][:, sl],
+                    out=banks[(hh, c)][:, 128 * j : 128 * (j + 1)],
+                    lhsT=xc[hh][:, pixels].bitcast(FP8X4),
+                    lhsT_scale=xs[hh][:, pixels],
                     rhs=wc[hw][:, kg, cols].bitcast(FP8X4),
                     rhs_scale=ws[hw][:, kg, cols],
                     start=(kg == 0),
                     stop=(kg == 1),
                 )
 
-        def stage1(hh, c):
-            if (hh, c) in begun:
-                bank = begun[(hh, c)]
-            else:
-                bank = new_bank("s1_%d_%d" % (hh, c))
-                for j in range(4):
-                    multiply(bank, hh, c, j)
-            on_gpsimd = c in GPSIMD_C[hh]
-            product = bank[:].rearrange("p (j w) -> p w j", j=4)
+        def shares_with_gpsimd(hh, turn):
+            return 0 < hh < HALVES - 1 or (hh, turn) == (HALVES - 1, 0)
+
+        def bias_add(hh, c):
+            product = banks[(hh, c)][:].rearrange("p (j w) -> p w j", j=4)
             bias_cols = bias[:, 128 * c : 128 * (c + 1)].unsqueeze(2).to_broadcast([P, 128, 4])
-            if on_gpsimd:
-                y = yp.tile([P, 512], F32, name="y%d_%d" % (hh, c), tag="y")
-                vg[(hh, c)] = yp.tile([P, 512], BF16, name="vg%d_%d" % (hh, c), tag="vg_gpsimd", align_bytes=64)
+            if c % 4 == 0 and shares_with_gpsimd(hh, c // 4):
+                y = gpsimd_pool.tile([P, 512], F32, name="y%d_%d" % (hh, c), tag="y")
                 y_grouped = y[:].rearrange("p (w j) -> p w j", j=4)
+                vg[(hh, c)] = gpsimd_pool.tile([P, 512], BF16, name="vg%d_%d" % (hh, c), tag="vg", align_bytes=64)
+                grouped = vg[(hh, c)][:].rearrange("p (w j) -> p w j", j=4)
                 nc.scalar.copy(out=y_grouped, in_=product)
-                nc.gpsimd.tensor_tensor(
-                    out=vg[(hh, c)][:].rearrange("p (w j) -> p w j", j=4), in0=y_grouped, in1=bias_cols, op=ADD
-                )
+                nc.gpsimd.tensor_tensor(out=grouped, in0=y_grouped, in1=bias_cols, op=ADD)
             else:
                 vg[(hh, c)] = vgp.tile([P, 512], BF16, name="vg%d_%d" % (hh, c), tag="vg", align_bytes=64)
-                nc.vector.tensor_tensor(
-                    out=vg[(hh, c)][:].rearrange("p (w j) -> p w j", j=4), in0=product, in1=bias_cols, op=ADD
-                )
+                grouped = vg[(hh, c)][:].rearrange("p (w j) -> p w j", j=4)
+                nc.vector.tensor_tensor(out=grouped, in0=product, in1=bias_cols, op=ADD)
 
         def quant_v(hh, c):
             h, q = divmod(c, 4)
@@ -244,11 +235,11 @@ def tile_text2imgca_pb_kernel(tc, beta, x2, Wv, bv, out):
         def stage2_pass(bank, b, nt, g, c0, c1):
             h = c0 // 4
             cols = slice(128 * (c0 - 4 * h), 128 * (c1 - 4 * h))
-            sl = slice(128 * (2 * g + nt), 128 * (2 * g + nt + 1))
+            rows = slice(128 * (2 * g + nt), 128 * (2 * g + nt + 1))
             nc.tensor.matmul_mx(
                 out=bank[:, 0 : 128 * (c1 - c0)],
-                lhsT=bc[b][:, sl].bitcast(FP8X4),
-                lhsT_scale=bs[b][:, sl],
+                lhsT=bc[b][:, rows].bitcast(FP8X4),
+                lhsT_scale=bs[b][:, rows],
                 rhs=vc[(2 * b + g, h)][:, cols].bitcast(FP8X4),
                 rhs_scale=vs[(2 * b + g, h)][:, cols],
                 start=(g == 0),
@@ -261,79 +252,87 @@ def tile_text2imgca_pb_kernel(tc, beta, x2, Wv, bv, out):
             copy(out=ot[:, 0:width], in_=bank[:, 0:width])
             nc.sync.dma_start(out=out[b, 128 * nt : 128 * (nt + 1), 128 * c0 : 128 * c1], in_=ot[:, 0:width])
 
-        def stage2(b, nt, c0, c1, copy):
+        def stage2(b, nt, c0, c1):
             bank = new_bank("s2_%d_%d_%d" % (b, nt, c0))
             stage2_pass(bank, b, nt, 0, c0, c1)
             stage2_pass(bank, b, nt, 1, c0, c1)
-            stage2_out(bank, b, nt, c0, c1, copy)
+            stage2_out(bank, b, nt, c0, c1, nc.scalar.copy)
 
         prepare_w(0)
-        keep_clock_up(WARM[1])
-        transpose_x(0, (0, 1, 2, 3))
+        keep_clock_up(WARM_X)
+        new_x(0)
+        transpose_x(0, (0, 1))
+        keep_clock_up(WARM_BETWEEN)
+        transpose_x(0, (2, 3))
         for j in range(4):
-            quant_x(0, j, parts=4)
-        for c in range(3):
-            begun[(0, c)] = new_bank("s1_0_%d" % c)
+            quant_x(0, j, 4)
+        for c in range(HEAD_GROUPS):
+            banks[(0, c)] = new_bank("s1_0_%d" % c)
         for j in range(4):
-            for c in range(3):
-                multiply(begun[(0, c)], 0, c, j)
-        for hh in range(6):
-            b, g = divmod(hh, 2)
+            for c in range(HEAD_GROUPS):
+                multiply(0, c, j)
+
+        for hh in range(HALVES):
             for c in range(8):
-                stage1(hh, c)
-                if hh == 0 and c == 1:
-                    prepare_w(1)
-                if g == 0 and b > 0:
+                turn, place = divmod(c, 4)
+                if (hh, c) not in banks:
+                    banks[(hh, c)] = new_bank("s1_%d_%d" % (hh, c))
+                    for j in range(4):
+                        multiply(hh, c, j)
+                bias_add(hh, c)
+
+                if hh >= 4 and 3 <= c <= 6:
+                    h, nt = divmod(c - 3, 2)
+                    stage2(hh - 4, nt, 4 * h, 4 * h + 4)
+                if hh == HALVES - 1 and c >= 6:
+                    stage2(BATCH - 1, c - 6, 0, 4)
+
+                if hh == 0:
+                    if c == 1:
+                        prepare_w(1)
                     if c == 3:
-                        stage2(b - 1, 0, 0, 4, nc.scalar.copy)
-                    if c == 4:
-                        stage2(b - 1, 1, 0, 4, nc.scalar.copy)
-                    if c == 5:
-                        stage2(b - 1, 0, 4, 8, nc.scalar.copy)
-                    if c == 6:
-                        stage2(b - 1, 1, 4, 8, nc.scalar.copy)
-                if hh == 5 and c >= 6:
-                    stage2(b, c - 6, 0, 4, nc.scalar.copy)
-                if hh == 0 and c == 3:
-                    transpose_x(1, (0, 1))
-                    keep_clock_up(WARM[3])
-                    transpose_x(1, (2, 3))
-                if c in (0, 2):
-                    if 0 < hh < 5:
+                        new_x(1)
+                        transpose_x(1, (0, 1))
+                        keep_clock_up(WARM_BETWEEN)
+                        transpose_x(1, (2, 3))
+                    if c in (3, 4):
+                        quant_x(1, c - 3, 2)
+                elif hh < HALVES - 1:
+                    if c == 0:
+                        new_x(hh + 1)
+                    if c in (0, 2):
                         transpose_x(hh + 1, (c, c + 1))
-                    if hh in BETA_AT:
-                        transpose_beta(BETA_AT[hh], (c // 2,))
-                if hh == 0 and c in (3, 4):
-                    quant_x(1, c - 3)
-                if 0 < hh < 5 and c == 3:
-                    quant_x(hh + 1, 0)
-                    quant_x(hh + 1, 1)
-                if hh in BETA_AT and c == 7:
-                    quant_beta(BETA_AT[hh])
-                if (hh, c) == (1, 3):
+                    if c == 3:
+                        quant_x(hh + 1, 0, 2)
+                        quant_x(hh + 1, 1, 2)
+
+                if place == 2 and 3 <= hh < 3 + BATCH - 1:
+                    turn_beta(hh - 3, turn)
+                if hh == 5 and c in (1, 2):
+                    turn_beta(2, c - 1)
+                if c == 7 and 3 <= hh < 3 + BATCH - 1 or (hh, c) == (5, 3):
+                    quant_beta(hh - 3)
+
+                if hh == 1 and place == 3:
                     for q in range(4):
-                        quant_v(0, q)
-                if (hh, c) == (1, 7):
-                    for q in range(4, 8):
-                        quant_v(0, q)
-                if any(q in GPSIMD_C[hh] for q in range(c - c % 4, c + 1)):
-                    if c % 4 == 3:
-                        for q in (c - 2, c - 1, c, c - 3):
-                            quant_v(hh, q)
+                        quant_v(0, 4 * turn + q)
+                if hh > 0 and shares_with_gpsimd(hh, turn):
+                    if place == 3:
+                        for q in (1, 2, 3, 0):
+                            quant_v(hh, 4 * turn + q)
                 elif hh > 0:
-                    if c % 4 > 0:
+                    if place > 0:
                         quant_v(hh, c - 1)
-                    if c % 4 == 3:
+                    if place == 3:
                         quant_v(hh, c)
+
         last = BATCH - 1
-        for nt in range(2):
-            stage2(last, nt, 4, 6, nc.scalar.copy)
-        for nt in range(2):
-            stage2(last, nt, 6, 7, nc.scalar.copy)
+        for c0, c1 in ((4, 6), (6, 7)):
+            for nt in range(2):
+                stage2(last, nt, c0, c1)
         end_banks = [new_bank("s2_end%d" % nt) for nt in range(2)]
-        for nt in range(2):
-            stage2_pass(end_banks[nt], last, nt, 0, 7, 8)
-        for nt in range(2):
-            stage2_pass(end_banks[nt], last, nt, 1, 7, 8)
+        for g in range(2):
+            for nt in range(2):
+                stage2_pass(end_banks[nt], last, nt, g, 7, 8)
         stage2_out(end_banks[0], last, 0, 7, 8, nc.scalar.copy)
         stage2_out(end_banks[1], last, 1, 7, 8, nc.vector.tensor_copy)

from contextlib import ExitStack

import concourse.mybir as mybir
from concourse.masks import make_identity

FLOPS = 2 * 3 * 1024 * 1024 * 1024 + 2 * 3 * 256 * 1024 * 1024

BF16 = mybir.dt.bfloat16
F32 = mybir.dt.float32
U32 = mybir.dt.uint32
U8 = mybir.dt.uint8
FP8X4 = mybir.dt.float8_e4m3fn_x4
ADD = mybir.AluOpType.add

P = 128
BATCH = 3
HALVES = 2 * BATCH
IC = 1024
TC = 1024

W_SPLIT = (352, 128)

WARM_BIAS, WARM_X, WARM_BETWEEN = 4, 6, 2

HEAD_GROUPS = 3


def tile_text2imgca_pb_kernel(tc, beta, x2, Wv, bv, out):
    nc = tc.nc
    x2p = x2.rearrange("b h w c -> b (h w) c")
    with ExitStack() as ctx:
        keep = ctx.enter_context(tc.tile_pool(name="keep", bufs=1))
        xgp = ctx.enter_context(tc.tile_pool(name="xgp", bufs=2))
        xcp = ctx.enter_context(tc.tile_pool(name="xcp", bufs=2))
        vgp = ctx.enter_context(tc.tile_pool(name="vgp", bufs=14))
        gpsimd_pool = ctx.enter_context(tc.tile_pool(name="gpsimd_pool", bufs=1))
        otp = ctx.enter_context(tc.tile_pool(name="otp", bufs=8))
        psum = ctx.enter_context(tc.psum_pool(name="psum", bufs=8))
        ctx.enter_context(tc.manual_schedule())

        def new_bank(name):
            return psum.tile([P, 512], F32, name=name, tag="bank")

        brow = keep.tile([P, TC], BF16, name="brow")
        nc.vector.memset(brow[:], 0.0)
        ones = keep.tile([P, P], BF16, name="ones")
        nc.vector.memset(ones[:], 1.0)
        ident = keep.tile([P, P], F32, name="ident")
        make_identity(nc, ident[:])
        idle_in = keep.tile([P, 512], BF16, name="idle_in")
        nc.vector.memset(idle_in[:], 0.0)
        idle_bank = new_bank("idle_bank")

        def keep_clock_up(count):
            for i in range(count):
                nc.tensor.matmul(out=idle_bank[:], lhsT=ones[:], rhs=idle_in[:], start=True, stop=True)

        wr = [keep.tile([P, 8, 512], BF16, name="wr%d" % hw) for hw in range(2)]
        xr = [keep.tile([P, 4, IC], BF16, name="xr%d" % hh) for hh in range(HALVES)]
        br = [keep.tile([P, 2, 16, 64], BF16, name="br%d" % b, align_bytes=64) for b in range(BATCH)]
        wv_rows = Wv.rearrange("(kk q ke) c -> q kk ke c", kk=4, ke=2)

        def load_w(hw, kk):
            nc.sync.dma_start(
                out=wr[hw][:, 2 * kk : 2 * kk + 2, :],
                in_=wv_rows[:, kk, :, 512 * hw : 512 * (hw + 1)],
            )

        def load_x(hh, pieces):
            b, g = divmod(hh, 2)
            rows = x2p[b, 512 * g : 512 * (g + 1), :]
            if pieces == 2:
                for u in range(2):
                    nc.sync.dma_start(
                        out=xr[hh][:, 2 * u : 2 * u + 2, :].rearrange("p e c -> p (e c)"),
                        in_=rows[256 * u : 256 * (u + 1), :].rearrange("(p e) c -> p (e c)", e=2),
                    )
            else:
                nc.sync.dma_start(
                    out=xr[hh][:].rearrange("p (u e) c -> p u (e c)", u=2),
                    in_=rows.rearrange("(u p e) c -> p u (e c)", u=2, e=2),
                )

        def load_beta(b):
            for g in range(2):
                for u in range(2):
                    for q in range(4):
                        k0 = 512 * g + 256 * u + 64 * q
                        nc.sync.dma_start(
                            out=br[b][32 * q + u : 32 * (q + 1) : 2, g, :, :],
                            in_=beta[b, :, k0 : k0 + 64].rearrange("(nh nl) k -> nl nh k", nl=16),
                        )

        load_w(0, 0)
        nc.sync.dma_start(out=brow[0:1, :], in_=bv.rearrange("(o c) -> o c", o=1))
        for kk in range(1, 4):
            load_w(0, kk)
        load_x(0, 2)
        for kk in range(4):
            load_w(1, kk)
        load_x(1, 2)
        load_x(2, 1)
        load_x(3, 1)
        load_beta(0)
        load_x(4, 1)
        load_beta(1)
        load_x(5, 1)
        load_beta(2)

        keep_clock_up(WARM_BIAS)
        bias = keep.tile([P, TC], F32, name="bias")
        for h in range(2):
            pb = new_bank("pb%d" % h)
            nc.tensor.matmul(out=pb[:], lhsT=ones[:], rhs=brow[:, 512 * h : 512 * (h + 1)], start=True, stop=True)
            nc.scalar.copy(out=bias[:, 512 * h : 512 * (h + 1)], in_=pb[:])

        wg = [keep.tile([P, 2, 512, 4], BF16, name="wg%d" % hw, align_bytes=64) for hw in range(2)]
        wc = [keep.tile([P, 2, 512], U32, name="wc%d" % hw, align_bytes=64) for hw in range(2)]
        ws = [keep.tile([P, 2, 512], U8, name="ws%d" % hw, align_bytes=64) for hw in range(2)]

        def regroup_w(hw, kg, c0, c1, copy):
            copy(
                out=wg[hw][:, kg, c0:c1, :].rearrange("p (c i) t -> p c t i", i=4),
                in_=wr[hw][:, 4 * kg : 4 * kg + 4, c0:c1].rearrange("p t (c i) -> p c t i", i=4),
            )

        def prepare_w(hw):
            for kg in range(2):
                regroup_w(hw, kg, 0, W_SPLIT[hw], nc.vector.tensor_copy)
                regroup_w(hw, kg, W_SPLIT[hw], 512, nc.scalar.copy)
            for kg in range(2):
                nc.vector.quantize_mx(
                    out=wc[hw][:, kg, :].bitcast(FP8X4),
                    scales=ws[hw][:, kg, :],
                    in_=wg[hw][:, kg, :, :].rearrange("p c t -> p (c t)"),
                )

        xg = {}
        xc = {}
        xs = {}

        def new_x(hh):
            xg[hh] = xgp.tile([P, 4096], BF16, name="xg%d" % hh, tag="xg", align_bytes=64)
            xc[hh] = xcp.tile([P, 1024], U32, name="xc%d" % hh, tag="xc", align_bytes=64)
            xs[hh] = xcp.tile([P, 1024], U8, name="xs%d" % hh, tag="xs", align_bytes=64)

        def transpose_x(hh, js):
            src = xr[hh][:].bitcast(F32)
            dst = xg[hh][:].bitcast(F32)
            for j in js:
                bank = new_bank("xt%d_%d" % (hh, j))
                for s in range(4):
                    nc.tensor.transpose(
                        out=bank[:, 128 * s : 128 * (s + 1)],
                        in_=src[:, j, 128 * s : 128 * (s + 1)],
                        identity=ident[:],
                    )
                nc.scalar.copy(
                    out=dst[:, 512 * j : 512 * (j + 1)].rearrange("p (kg r ku) -> p kg r ku", kg=2, ku=2),
                    in_=bank[:].rearrange("p (kg ku r) -> p kg r ku", kg=2, ku=2),
                )

        def quant_x(hh, part, parts):
            width = 1024 // parts
            cols = slice(width * part, width * (part + 1))
            nc.vector.quantize_mx(
                out=xc[hh][:, cols].bitcast(FP8X4),
                scales=xs[hh][:, cols],
                in_=xg[hh][:, 4 * width * part : 4 * width * (part + 1)],
            )

        bg = [keep.tile([P, 2048], BF16, name="bg%d" % b, align_bytes=64) for b in range(BATCH)]
        bc = [keep.tile([P, 512], U32, name="bc%d" % b, align_bytes=64) for b in range(BATCH)]
        bs = [keep.tile([P, 512], U8, name="bs%d" % b, align_bytes=64) for b in range(BATCH)]

        def turn_beta(b, g):
            nc.vector.transpose(
                out=bg[b][:].bitcast(F32)[:, 512 * g : 512 * (g + 1)],
                in_=br[b][:].rearrange("p g nh k -> p (g nh k)").bitcast(F32)[:, 512 * g : 512 * (g + 1)],
            )

        def quant_beta(b):
            nc.vector.quantize_mx(out=bc[b][:].bitcast(FP8X4), scales=bs[b][:], in_=bg[b][:])

        banks = {}
        vg = {}
        vc = {}
        vs = {}
        for hh in range(HALVES):
            for h in range(2):
                vc[(hh, h)] = keep.tile([P, 512], U32, name="vc%d_%d" % (hh, h), align_bytes=64)
                vs[(hh, h)] = keep.tile([P, 512], U8, name="vs%d_%d" % (hh, h), align_bytes=64)

        def multiply(hh, c, j):
            hw, q = divmod(c, 4)
            cols = slice(128 * q, 128 * (q + 1))
            for kg in range(2):
                pixels = slice(128 * (2 * j + kg), 128 * (2 * j + kg + 1))
                nc.tensor.matmul_mx(
                    out=banks[(hh, c)][:, 128 * j : 128 * (j + 1)],
                    lhsT=xc[hh][:, pixels].bitcast(FP8X4),
                    lhsT_scale=xs[hh][:, pixels],
                    rhs=wc[hw][:, kg, cols].bitcast(FP8X4),
                    rhs_scale=ws[hw][:, kg, cols],
                    start=(kg == 0),
                    stop=(kg == 1),
                )

        def shares_with_gpsimd(hh, turn):
            return 0 < hh < HALVES - 1 or (hh, turn) == (HALVES - 1, 0)

        def bias_add(hh, c):
            product = banks[(hh, c)][:].rearrange("p (j w) -> p w j", j=4)
            bias_cols = bias[:, 128 * c : 128 * (c + 1)].unsqueeze(2).to_broadcast([P, 128, 4])
            if c % 4 == 0 and shares_with_gpsimd(hh, c // 4):
                y = gpsimd_pool.tile([P, 512], F32, name="y%d_%d" % (hh, c), tag="y")
                y_grouped = y[:].rearrange("p (w j) -> p w j", j=4)
                vg[(hh, c)] = gpsimd_pool.tile([P, 512], BF16, name="vg%d_%d" % (hh, c), tag="vg", align_bytes=64)
                grouped = vg[(hh, c)][:].rearrange("p (w j) -> p w j", j=4)
                nc.scalar.copy(out=y_grouped, in_=product)
                nc.gpsimd.tensor_tensor(out=grouped, in0=y_grouped, in1=bias_cols, op=ADD)
            else:
                vg[(hh, c)] = vgp.tile([P, 512], BF16, name="vg%d_%d" % (hh, c), tag="vg", align_bytes=64)
                grouped = vg[(hh, c)][:].rearrange("p (w j) -> p w j", j=4)
                nc.vector.tensor_tensor(out=grouped, in0=product, in1=bias_cols, op=ADD)

        def quant_v(hh, c):
            h, q = divmod(c, 4)
            nc.vector.quantize_mx(
                out=vc[(hh, h)][:, 128 * q : 128 * (q + 1)].bitcast(FP8X4),
                scales=vs[(hh, h)][:, 128 * q : 128 * (q + 1)],
                in_=vg[(hh, c)][:],
            )

        def stage2_pass(bank, b, nt, g, c0, c1):
            h = c0 // 4
            cols = slice(128 * (c0 - 4 * h), 128 * (c1 - 4 * h))
            rows = slice(128 * (2 * g + nt), 128 * (2 * g + nt + 1))
            nc.tensor.matmul_mx(
                out=bank[:, 0 : 128 * (c1 - c0)],
                lhsT=bc[b][:, rows].bitcast(FP8X4),
                lhsT_scale=bs[b][:, rows],
                rhs=vc[(2 * b + g, h)][:, cols].bitcast(FP8X4),
                rhs_scale=vs[(2 * b + g, h)][:, cols],
                start=(g == 0),
                stop=(g == 1),
            )

        def stage2_out(bank, b, nt, c0, c1, copy):
            width = 128 * (c1 - c0)
            ot = otp.tile([P, 512], F32, name="ot%d_%d_%d" % (b, nt, c0), tag="ot")
            copy(out=ot[:, 0:width], in_=bank[:, 0:width])
            nc.sync.dma_start(out=out[b, 128 * nt : 128 * (nt + 1), 128 * c0 : 128 * c1], in_=ot[:, 0:width])

        def stage2(b, nt, c0, c1):
            bank = new_bank("s2_%d_%d_%d" % (b, nt, c0))
            stage2_pass(bank, b, nt, 0, c0, c1)
            stage2_pass(bank, b, nt, 1, c0, c1)
            stage2_out(bank, b, nt, c0, c1, nc.scalar.copy)

        prepare_w(0)
        keep_clock_up(WARM_X)
        new_x(0)
        transpose_x(0, (0, 1))
        keep_clock_up(WARM_BETWEEN)
        transpose_x(0, (2, 3))
        for j in range(4):
            quant_x(0, j, 4)
        for c in range(HEAD_GROUPS):
            banks[(0, c)] = new_bank("s1_0_%d" % c)
        for j in range(4):
            for c in range(HEAD_GROUPS):
                multiply(0, c, j)

        for hh in range(HALVES):
            for c in range(8):
                turn, place = divmod(c, 4)
                if (hh, c) not in banks:
                    banks[(hh, c)] = new_bank("s1_%d_%d" % (hh, c))
                    for j in range(4):
                        multiply(hh, c, j)
                bias_add(hh, c)

                if hh >= 4 and 3 <= c <= 6:
                    h, nt = divmod(c - 3, 2)
                    stage2(hh - 4, nt, 4 * h, 4 * h + 4)
                if hh == HALVES - 1 and c >= 6:
                    stage2(BATCH - 1, c - 6, 0, 4)

                if hh == 0:
                    if c == 1:
                        prepare_w(1)
                    if c == 3:
                        new_x(1)
                        transpose_x(1, (0, 1))
                        keep_clock_up(WARM_BETWEEN)
                        transpose_x(1, (2, 3))
                    if c in (3, 4):
                        quant_x(1, c - 3, 2)
                elif hh < HALVES - 1:
                    if c == 0:
                        new_x(hh + 1)
                    if c in (0, 2):
                        transpose_x(hh + 1, (c, c + 1))
                    if c == 3:
                        quant_x(hh + 1, 0, 2)
                        quant_x(hh + 1, 1, 2)

                if place == 2 and 3 <= hh < 3 + BATCH - 1:
                    turn_beta(hh - 3, turn)
                if hh == 5 and c in (1, 2):
                    turn_beta(2, c - 1)
                if c == 7 and 3 <= hh < 3 + BATCH - 1 or (hh, c) == (5, 3):
                    quant_beta(hh - 3)

                if hh == 1 and place == 3:
                    for q in range(4):
                        quant_v(0, 4 * turn + q)
                if hh > 0 and shares_with_gpsimd(hh, turn):
                    if place == 3:
                        for q in (1, 2, 3, 0):
                            quant_v(hh, 4 * turn + q)
                elif hh > 0:
                    if place > 0:
                        quant_v(hh, c - 1)
                    if place == 3:
                        quant_v(hh, c)

        last = BATCH - 1
        for c0, c1 in ((4, 6), (6, 7)):
            for nt in range(2):
                stage2(last, nt, c0, c1)
        end_banks = [new_bank("s2_end%d" % nt) for nt in range(2)]
        for g in range(2):
            for nt in range(2):
                stage2_pass(end_banks[nt], last, nt, g, 7, 8)
        stage2_out(end_banks[0], last, 0, 7, 8, nc.scalar.copy)
        stage2_out(end_banks[1], last, 1, 7, 8, nc.vector.tensor_copy)
